import numpy as np
import ml_dtypes


def mxq(x, axis, fmt="e4m3"):
    dtype, down = {"e4m3": (ml_dtypes.float8_e4m3fn, 7), "e5m2": (ml_dtypes.float8_e5m2, 14)}[fmt]
    v = np.moveaxis(np.asarray(x, np.float32).astype(ml_dtypes.bfloat16).astype(np.float64), axis, -1)
    blocks = v.reshape(v.shape[:-1] + (-1, 32))
    amax = np.abs(blocks).max(-1, keepdims=True)
    byte = np.maximum(np.where(amax > 0, np.frexp(amax)[1] - 1 + 127, 0) - down, 1)
    scale = np.exp2(byte - 127.0)
    codes = (blocks / scale).astype(np.float32).astype(dtype).astype(np.float64)
    return np.moveaxis((codes * scale).reshape(v.shape), -1, axis)


WIDE = False


def mx_kscale(k):
    if not WIDE:
        return np.ones(k)
    levels = np.array([10, -10, 5, -5, 0])
    if k % 512:
        return np.exp2(np.random.permutation(np.resize(levels, k // 32))).repeat(32)
    a = np.empty((k // 512, 16))
    for p in range(k // 512):
        a[p, :8] = np.random.permutation(np.resize(levels, 8))
        for g in range(8):
            far = levels[np.abs(levels - a[p, g]) >= 10]
            a[p, g + 8] = far[np.random.randint(len(far))]
    return np.exp2(a.ravel()).repeat(32)


BF16 = ml_dtypes.bfloat16


def bf(x):
    return np.asarray(x, np.float32).astype(BF16)


def f64(x):
    return np.asarray(x).astype(np.float64)


E2M1 = np.array([0.0, 0.5, 1.0, 1.5, 2.0, 3.0, 4.0, 6.0, -0.0, -0.5, -1.0, -1.5, -2.0, -3.0, -4.0, -6.0])


def pack_weight(w, fmt):
    k, n = w.shape
    w = f64(bf(w)).reshape(k // 32, 32, n)
    amax = np.abs(w).max(1)
    if fmt == "e4m3":
        byte = np.frexp(amax)[1] - 1 + 127 - 7
    else:
        mant, ex = np.frexp(amax / 6.0)
        byte = np.where(mant > 0.5, ex, ex - 1) + 127
    byte = np.clip(np.where(amax > 0, byte, 1), 1, 254)
    scaled = (w * np.exp2(127.0 - byte)[:, None, :]).reshape(k, n).astype(np.float32)
    by_word = np.ascontiguousarray(scaled.reshape(k // 512, 128, 4, n).transpose(0, 1, 3, 2))
    if fmt == "e4m3":
        words = by_word.astype(ml_dtypes.float8_e4m3fn).view(np.uint8)
    else:
        c = by_word.astype(ml_dtypes.float4_e2m1fn).view(np.uint8) & 0xF
        words = c[..., 0::2] | (c[..., 1::2] << 4)
    return np.ascontiguousarray(words), np.ascontiguousarray(byte.astype(np.uint8).reshape(k // 512, 16, n))


def unpack_weight(words, scales, fmt):
    g, p, n, _ = words.shape
    if fmt == "e4m3":
        vals = np.ascontiguousarray(words).view(ml_dtypes.float8_e4m3fn).astype(np.float64)
    else:
        nib = np.empty((g, p, n, 4), np.uint8)
        nib[..., 0::2] = words & 0xF
        nib[..., 1::2] = words >> 4
        vals = E2M1[nib]
    vals = vals * np.repeat(np.exp2(scales.astype(np.float64) - 127.0), 8, axis=1)[..., None]
    return vals.transpose(0, 1, 3, 2).reshape(g * 512, n)
def pack4(w):
    words, scales = pack_weight(w, "e2m1")
    return words.reshape(words.shape[0], 128, -1), scales


def unpack4(words, scales):
    return unpack_weight(words.reshape(words.shape[0], 128, -1, 2), scales, "e2m1")


B, S, DIM, KV, H = 4, 128, 2048, 512, 16
HD = DIM // H
G = 0.6 * DIM ** 0.25


def heads(v):
    return v.reshape(B, S, H, HD).transpose(0, 2, 1, 3)


def rope(v, cos, sin):
    vr, vi = v[..., 0::2], v[..., 1::2]
    return np.stack([vr * cos - vi * sin, vr * sin + vi * cos], axis=-1).reshape(v.shape)


def draw0():
    s, u = mx_kscale(DIM), mx_kscale(KV)
    ang = np.outer(np.arange(S), 1.0 / 10000.0 ** (np.arange(0, HD, 2) / HD))
    x = bf(np.random.standard_normal((B, S, DIM)) * s)
    W_kv_down_words, W_kv_down_scales = pack4((np.random.standard_normal((KV, DIM)) / np.sqrt(DIM) * u[:, None] / s).T)
    b_kv_down = bf(np.random.standard_normal(KV) * 0.3 * u)
    Wq_words, Wq_scales = pack4((np.random.standard_normal((DIM, DIM)) * G / np.sqrt(DIM) / s).T)
    bq = bf(np.random.standard_normal(DIM) * 0.2 * G)
    W_uk_words, W_uk_scales = pack4((np.random.standard_normal((DIM, KV)) * G / np.sqrt(KV) / u).T)
    b_uk = bf(np.random.standard_normal(DIM) * 0.2 * G)
    return {"x": x,
            "rope_cos": bf(np.cos(ang)),
            "rope_sin": bf(np.sin(ang)),
            "W_kv_down_words": W_kv_down_words,
            "W_kv_down_scales": W_kv_down_scales,
            "b_kv_down": b_kv_down,
            "Wq_words": Wq_words,
            "Wq_scales": Wq_scales,
            "bq": bq,
            "W_uk_words": W_uk_words,
            "W_uk_scales": W_uk_scales,
            "b_uk": b_uk}


def core(x, rope_cos, rope_sin, W_kv_down_words, W_kv_down_scales, b_kv_down, Wq_words, Wq_scales, bq, W_uk_words, W_uk_scales, b_uk):
    cos, sin = f64(rope_cos), f64(rope_sin)
    xq = mxq(f64(x), 2, "e4m3")
    l_kv = (xq @ unpack4(W_kv_down_words, W_kv_down_scales)) + f64(b_kv_down)
    q = (xq @ unpack4(Wq_words, Wq_scales)) + f64(bq)
    k = (mxq(l_kv, 2, "e4m3") @ unpack4(W_uk_words, W_uk_scales)) + f64(b_uk)
    q_rot = rope(heads(q), cos, sin)
    k_rot = rope(heads(k), cos, sin)
    z = q_rot * k_rot * DIM ** (-0.5)
    e = np.exp(z - z.max(-1, keepdims=True))
    return e / e.sum(-1, keepdims=True)


def e4m3fn_bytes(y):
    return np.clip(np.asarray(y, np.float64), -448.0, 448.0).astype(np.float32).astype(ml_dtypes.float8_e4m3fn).view(np.uint8)


def e4m3fn_values(b):
    return np.asarray(b, np.uint8).view(ml_dtypes.float8_e4m3fn).astype(np.float64)


def setup_inputs():
    d = draw0()
    x0 = np.asarray(d['x']).astype(np.float64)
    s = (np.max(np.abs(x0), axis=(0, 1), keepdims=True) / 448.0).astype(np.float32)
    out = {}
    for k, v in d.items():
        if k == 'x':
            out['x_bytes'] = e4m3fn_bytes(x0 / s.astype(np.float64))
            out['x_scale'] = s
        else:
            out[k] = v
    return out


def reference(x_bytes, x_scale, rope_cos, rope_sin, W_kv_down_words, W_kv_down_scales, b_kv_down, Wq_words, Wq_scales, bq, W_uk_words, W_uk_scales, b_uk):
    return core(e4m3fn_values(x_bytes) * x_scale.astype(np.float64), rope_cos, rope_sin, W_kv_down_words, W_kv_down_scales, b_kv_down, Wq_words, Wq_scales, bq, W_uk_words, W_uk_scales, b_uk)

from contextlib import ExitStack

import concourse.mybir as mybir
from concourse.masks import make_identity

F32 = mybir.dt.float32
BF16 = mybir.dt.bfloat16
I32 = mybir.dt.int32
U32 = mybir.dt.uint32
U8 = mybir.dt.uint8
FP8 = mybir.dt.float8_e4m3fn
FP8X4 = mybir.dt.float8_e4m3fn_x4
FP4X4 = mybir.dt.float4_e2m1fn_x4
ALU = mybir.AluOpType
ACT = mybir.ActivationFunctionType
AX = mybir.AxisListType

B, S, DIM, KV, H, HD = 4, 128, 2048, 512, 16, 128
P = 128
G = DIM // 512
T = B * S
FLOPS = 2 * T * (DIM * DIM + DIM * KV + KV * DIM)
KAPPA = DIM ** -0.5


def tile_multilatentattention_pa_w4_kernel(
    tc, x_bytes, x_scale, rope_cos, rope_sin, W_kv_down_words, W_kv_down_scales, b_kv_down,
    Wq_words, Wq_scales, bq, W_uk_words, W_uk_scales, b_uk, out,
):
    nc = tc.nc
    with ExitStack() as ctx:
        keep = ctx.enter_context(tc.tile_pool(name="keep", bufs=1))
        work = ctx.enter_context(tc.tile_pool(name="work", bufs=2))
        psum = ctx.enter_context(tc.psum_pool(name="psum", bufs=2))
        ctx.enter_context(tc.manual_schedule())

        def bank(tag, shape):
            t = psum.tile(shape, F32, tag=tag, name=tag)
            return t

        ident = keep.tile([P, P], F32, name="ident")
        perm = keep.tile([P, P], F32, name="perm")
        xs_rows = keep.tile([P, P], F32, name="xs_rows")
        vec_rows = keep.tile([P, P], BF16, name="vec_rows")
        vec_f32 = keep.tile([P, P], F32, name="vec_f32")
        cs_raw = keep.tile([P, 2, HD // 2], BF16, name="cs_raw")
        cs_wide = keep.tile([P, 2, HD], F32, name="cs_wide")
        xs_cols = keep.tile([P, DIM // P], F32, name="xs_cols")
        xs_all = keep.tile([P, DIM], F32, name="xs_all")
        vec_cols = keep.tile([P, P], F32, name="vec_cols")
        rope_t = keep.tile([P, 2, S], F32, name="rope_t")
        bkv_all = keep.tile([P, KV], F32, name="bkv_all")
        warm = keep.tile([P, 1], F32, name="warm")
        wkv = keep.tile([P, G, 2 * KV], U8, name="wkv", align_bytes=256)
        wkv_s = keep.tile([P, G, KV], U8, name="wkv_s", align_bytes=256)
        wq = keep.tile([P, G, 2 * DIM], U8, name="wq", align_bytes=256)
        wq_s = keep.tile([P, G, DIM], U8, name="wq_s", align_bytes=256)
        wuk = keep.tile([P, 2 * DIM], U8, name="wuk", align_bytes=256)
        wuk_s = keep.tile([P, DIM], U8, name="wuk_s", align_bytes=256)
        xq = keep.tile([P, G, T], U32, name="xq", align_bytes=256)
        xq_s = keep.tile([P, G, T], U8, name="xq_s", align_bytes=256)
        lq = keep.tile([P, T], U32, name="lq", align_bytes=256)
        lq_s = keep.tile([P, T], U8, name="lq_s", align_bytes=256)
        x_codes = [keep.tile([P, DIM], U8, name="x_codes%d" % b, align_bytes=64) for b in range(B)]

        make_identity(nc, ident[:])
        nc.vector.memset(xs_rows[:], 0.0)
        nc.vector.memset(vec_rows[:], 0.0)
        nc.vector.memset(warm[:], 0.0)
        nc.vector.memset(wkv_s[:].rearrange("p g n -> p (g n)").bitcast(I32), 0)
        nc.vector.memset(wq_s[:].rearrange("p g n -> p (g n)").bitcast(I32), 0)
        nc.vector.memset(wuk_s[:].bitcast(I32), 0)

        nc.sync.dma_start(out=xs_rows[0 : DIM // P, :], in_=x_scale.rearrange("a b (r c) -> (a b r) c", c=P))
        nc.scalar.dma_start(out=vec_rows[0:16, :], in_=bq.rearrange("(r c) -> r c", c=P))
        nc.scalar.dma_start(out=vec_rows[32:48, :], in_=b_uk.rearrange("(r c) -> r c", c=P))
        nc.scalar.dma_start(out=vec_rows[64:68, :], in_=b_kv_down.rearrange("(r c) -> r c", c=P))
        nc.scalar.dma_start(out=cs_raw[:, 0, :], in_=rope_cos)
        nc.scalar.dma_start(out=cs_raw[:, 1, :], in_=rope_sin)
        nc.scalar.activation(out=warm[:], in_=warm[:], func=ACT.Exp)

        def load_x(b):
            nc.sync.dma_start(out=x_codes[b][:], in_=x_bytes[b])

        def load_scales(dst, src, groups, n):
            view = dst.bitcast(I32).rearrange("p (g n) -> p g n", g=groups)
            for quad in range(4):
                nc.sync.dma_start(
                    out=view[32 * quad : 32 * quad + 4, :, :],
                    in_=src[:, 4 * quad : 4 * quad + 4, :].bitcast(I32).rearrange("g r n -> r g n"),
                )

        load_x(0)
        load_x(1)
        load_scales(wkv_s[:].rearrange("p g n -> p (g n)"), W_kv_down_scales, G, KV)
        load_scales(wq_s[:].rearrange("p g n -> p (g n)"), Wq_scales, G, DIM)
        load_scales(wuk_s[:], W_uk_scales, 1, DIM)
        load_x(2)
        nc.sync.dma_start(out=wkv[:], in_=W_kv_down_words.rearrange("g p n -> p g n"))
        load_x(3)
        for g in range(G):
            nc.sync.dma_start(out=wq[:, g, :], in_=Wq_words[g])
        nc.sync.dma_start(out=wuk[:], in_=W_uk_words[0])

        pv = perm[:].rearrange("p (i r) -> p i r", r=2)
        iv = ident[:].rearrange("p (i r) -> p i r", r=2)
        nc.vector.tensor_copy(out=pv[:, :, 0], in_=iv[:, :, 1])
        nc.vector.tensor_copy(out=pv[:, :, 1], in_=iv[:, :, 0])

        xs_ps = bank("ut", [P, P])
        nc.tensor.transpose(xs_ps[:], xs_rows[:], ident[:])
        nc.scalar.copy(out=xs_cols[:], in_=xs_ps[:, 0 : DIM // P])
        for j, tag in enumerate(("qf", "qf", "kf", "kf")):
            sp = bank(tag, [P, 512])
            for i in range(4):
                r = 4 * j + i
                nc.tensor.transpose(sp[:, P * i : P * i + P], xs_cols[:, r : r + 1].to_broadcast([P, P]), ident[:])
            nc.scalar.copy(out=xs_all[:, 512 * j : 512 * j + 512], in_=sp[:])

        nc.vector.tensor_copy(out=vec_f32[:], in_=vec_rows[:])
        csw = cs_wide[:].rearrange("p a (i r) -> p a i r", r=2)
        for r in range(2):
            nc.vector.tensor_copy(out=csw[:, 0, :, r], in_=cs_raw[:, 0, :])
            nc.vector.tensor_scalar(
                out=csw[:, 1, :, r], in0=cs_raw[:, 1, :], scalar1=1.0 - 2.0 * r, scalar2=None, op0=ALU.mult
            )
        small_ps = bank("vt", [P, 3, P])
        nc.tensor.transpose(small_ps[:, 0, :], vec_f32[:], ident[:])
        nc.tensor.transpose(small_ps[:, 1, :], cs_wide[:, 0, :], ident[:])
        nc.tensor.transpose(small_ps[:, 2, :], cs_wide[:, 1, :], ident[:])
        nc.scalar.copy(out=vec_cols[:], in_=small_ps[:, 0, :])
        nc.scalar.copy(out=rope_t[:], in_=small_ps[:, 1:3, :])
        bkv_ps = bank("ut", [P, KV])
        for r in range(4):
            nc.tensor.transpose(bkv_ps[:, P * r : P * r + P], vec_cols[:, 64 + r : 65 + r].to_broadcast([P, P]), ident[:])
        nc.scalar.copy(out=bkv_all[:], in_=bkv_ps[:])

        cos_b = rope_t[:, 0, :].unsqueeze(1).to_broadcast([P, B, S])
        sin_b = rope_t[:, 1, :].unsqueeze(1).to_broadcast([P, B, S])

        xb_tiles = {}
        grp_tiles = {}

        def widen(b, lo, hi):
            if lo == 0:
                xb_tiles[b] = work.tile([P, DIM], BF16, tag="xb", name="xb", align_bytes=64)
            nc.vector.tensor_tensor(
                out=xb_tiles[b][:, lo:hi], in0=x_codes[b][:, lo:hi].bitcast(FP8), in1=xs_all[:, lo:hi], op=ALU.mult
            )

        def turn(b, half):
            if half == 0:
                grp_tiles[b] = work.tile([P, G, S, 4], BF16, tag="grp", name="grp", align_bytes=64)
            words = xb_tiles[b][:].bitcast(F32)
            xt = bank(("ut", "vt")[half], [P, 2, 2, S])
            for gg in range(2):
                g = 2 * half + gg
                for u in range(2):
                    nc.tensor.transpose(xt[:, gg, u, :], words[:, 256 * g + u : 256 * (g + 1) : 2], ident[:])
            nc.scalar.copy(
                out=grp_tiles[b][:, 2 * half : 2 * half + 2, :, :].bitcast(F32), in_=xt[:].rearrange("p g u r -> p g r u")
            )

        def quant_x(b):
            cols = slice(b * S, b * S + S)
            for g in range(G):
                nc.vector.quantize_mx(
                    out=xq[:, g, cols].bitcast(FP8X4),
                    scales=xq_s[:, g, cols],
                    in_=grp_tiles[b][:, g, :, :].rearrange("p r t -> p (r t)"),
                )

        l_ps = {}
        lb_tiles = {}
        lg_tiles = {}

        def mm_l(b):
            l_ps[b] = bank("kf", [P, KV])
            cols = slice(b * S, b * S + S)
            for g in range(G):
                nc.tensor.matmul_mx(
                    out=l_ps[b][:],
                    lhsT=xq[:, g, cols].bitcast(FP8X4),
                    lhsT_scale=xq_s[:, g, cols],
                    rhs=wkv[:, g, :].bitcast(FP4X4),
                    rhs_scale=wkv_s[:, g, :],
                    start=(g == 0),
                    stop=(g == G - 1),
                )

        def bias_l(b):
            lb_tiles[b] = work.tile([P, KV], BF16, tag="lb", name="lb", align_bytes=64)
            nc.vector.tensor_tensor(out=lb_tiles[b][:], in0=l_ps[b][:], in1=bkv_all[:], op=ALU.add)

        def turn_l(b):
            lg_tiles[b] = work.tile([P, S, 4], BF16, tag="lg", name="lg", bufs=4, align_bytes=64)
            words = lb_tiles[b][:].bitcast(F32)
            lt = bank(("ut", "vt")[b % 2], [P, 2, S])
            for u in range(2):
                nc.tensor.transpose(lt[:, u, :], words[:, u:256:2], ident[:])
            nc.scalar.copy(out=lg_tiles[b][:].bitcast(F32), in_=lt[:].rearrange("p u r -> p r u"))

        def quant_l(b):
            cols = slice(b * S, b * S + S)
            nc.vector.quantize_mx(
                out=lq[:, cols].bitcast(FP8X4), scales=lq_s[:, cols], in_=lg_tiles[b][:].rearrange("p r t -> p (r t)")
            )

        qf, kf, uf, p1q, p2q, p1k, p2k, ut, vt, us, nz, nm, ee, sm, rc = ({} for n in range(15))

        def wtile(name, bufs, shape=(P, B, S)):
            t = work.tile(list(shape), F32, tag=name, name=name, bufs=bufs)
            return t

        def mm_q(h):
            qf[h] = bank("qf", [P, T])
            for g in range(G):
                nc.tensor.matmul_mx(
                    out=qf[h][:],
                    lhsT=wq[:, g, 2 * HD * h : 2 * HD * (h + 1)].bitcast(FP4X4),
                    lhsT_scale=wq_s[:, g, HD * h : HD * (h + 1)],
                    rhs=xq[:, g, :].bitcast(FP8X4),
                    rhs_scale=xq_s[:, g, :],
                    start=(g == 0),
                    stop=(g == G - 1),
                )

        def mm_k(h):
            kf[h] = bank("kf", [P, T])
            nc.tensor.matmul_mx(
                out=kf[h][:],
                lhsT=wuk[:, 2 * HD * h : 2 * HD * (h + 1)].bitcast(FP4X4),
                lhsT_scale=wuk_s[:, HD * h : HD * (h + 1)],
                rhs=lq[:].bitcast(FP8X4),
                rhs_scale=lq_s[:],
                start=True,
                stop=True,
            )

        def biased_times(dst, src, bias, table):
            nc.vector.scalar_tensor_tensor(
                out=dst[:], in0=src[:].rearrange("p (b s) -> p b s", b=B), scalar=bias, in1=table, op0=ALU.add, op1=ALU.mult
            )

        def k_cos(h):
            p1k[h] = wtile("p1k", 2)
            biased_times(p1k[h], kf[h], vec_cols[:, 32 + h : 33 + h], cos_b)

        def k_sin(h):
            p2k[h] = wtile("p2k", 2)
            biased_times(p2k[h], kf[h], vec_cols[:, 32 + h : 33 + h], sin_b)

        def q_cos(h):
            p1q[h] = wtile("p1q", 2)
            biased_times(p1q[h], qf[h], vec_cols[:, h : h + 1], cos_b)

        def q_out(h):
            uf[h] = wtile("uf", 2)
            nc.scalar.activation(
                out=uf[h][:], in_=qf[h][:].rearrange("p (b s) -> p b s", b=B), func=ACT.Identity, bias=vec_cols[:, h : h + 1], scale=1.0
            )

        def q_sin(h):
            p2q[h] = wtile("p2q", 2)
            nc.gpsimd.tensor_tensor(out=p2q[h][:], in0=uf[h][:], in1=sin_b, op=ALU.mult)

        def rotate(dst, a, c):
            for b in range(B):
                cols = slice(b * S, b * S + S)
                nc.tensor.matmul(out=dst[:, cols], lhsT=a[:, b, :], rhs=ident[:], start=True, stop=False, is_transpose=True)
                nc.tensor.matmul(out=dst[:, cols], lhsT=c[:, b, :], rhs=perm[:], start=False, stop=True, is_transpose=True)

        def rot_q(h):
            ut[h] = bank("ut", [P, T])
            rotate(ut[h], p1q[h], p2q[h])

        def rot_k(h):
            vt[h] = bank("vt", [P, T])
            rotate(vt[h], p1k[h], p2k[h])

        def q_scaled(h):
            us[h] = wtile("us", 2, (P, T))
            nc.scalar.activation(out=us[h][:], in_=ut[h][:], func=ACT.Copy, scale=-KAPPA)

        def product(h):
            nz[h] = wtile("nz", 3)
            nc.vector.tensor_tensor(out=nz[h][:].rearrange("p b d -> p (b d)"), in0=vt[h][:], in1=us[h][:], op=ALU.mult)

        def neg_max(h):
            nm[h] = wtile("nm", 3, (P, B))
            nc.vector.tensor_reduce(out=nm[h][:], in_=nz[h][:], axis=AX.X, op=ALU.min)

        def expo(h):
            ee[h] = wtile("ee", 3)
            sm[h] = wtile("sm", 3, (P, B))
            for b in range(B):
                nc.scalar.activation(
                    out=ee[h][:, b, :], in_=nz[h][:, b, :], func=ACT.Exp, scale=-1.0, bias=nm[h][:, b : b + 1], accum_out=sm[h][:, b : b + 1]
                )

        def recip(h):
            rc[h] = wtile("rc", 3, (P, B))
            nc.vector.reciprocal(out=rc[h][:], in_=sm[h][:])

        def norm_store(h):
            on = wtile("on", 3)
            for b in range(B):
                nc.scalar.activation(out=on[:, b, :], in_=ee[h][:, b, :], func=ACT.Copy, scale=rc[h][:, b : b + 1])
            nc.sync.dma_start(out=out[:, h].rearrange("b s d -> s b d"), in_=on[:])

        for c in range(4):
            widen(0, 512 * c, 512 * c + 512)
        turn(0, 0)
        turn(0, 1)
        widen(1, 0, 1024)
        widen(1, 1024, 2048)
        quant_x(0)
        turn(1, 0)
        turn(1, 1)
        widen(2, 0, 1024)
        widen(2, 1024, 2048)
        quant_x(1)
        mm_l(0)
        turn(2, 0)
        turn(2, 1)
        widen(3, 0, 1024)
        widen(3, 1024, 2048)
        bias_l(0)
        quant_x(2)
        mm_l(1)
        turn(3, 0)
        turn(3, 1)
        bias_l(1)
        quant_x(3)
        turn_l(0)
        turn_l(1)
        mm_l(2)
        bias_l(2)
        mm_l(3)
        quant_l(0)
        bias_l(3)
        quant_l(1)
        mm_q(0)
        turn_l(2)
        turn_l(3)
        quant_l(2)
        quant_l(3)

        for step in range(H + 4):
            h = step
            live = h < H
            if live:
                mm_k(h)
                if h > 0:
                    mm_q(h)
            if 0 <= h - 2 < H:
                product(h - 2)
            if 0 <= h - 3 < H:
                expo(h - 3)
            if 0 <= h - 4 < H:
                norm_store(h - 4)
            if live:
                k_cos(h)
            if 0 <= h - 2 < H:
                neg_max(h - 2)
            if live:
                q_out(h)
                k_sin(h)
                q_cos(h)
                q_sin(h)
            if 0 <= h - 1 < H:
                rot_q(h - 1)
                q_scaled(h - 1)
                rot_k(h - 1)
            if 0 <= h - 3 < H:
                recip(h - 3)
